import numpy as np
import ml_dtypes


def mxq(x, axis, fmt="e4m3"):
    dtype, down = {"e4m3": (ml_dtypes.float8_e4m3fn, 7), "e5m2": (ml_dtypes.float8_e5m2, 14)}[fmt]
    v = np.moveaxis(np.asarray(x, np.float32).astype(ml_dtypes.bfloat16).astype(np.float64), axis, -1)
    blocks = v.reshape(v.shape[:-1] + (-1, 32))
    amax = np.abs(blocks).max(-1, keepdims=True)
    byte = np.maximum(np.where(amax > 0, np.frexp(amax)[1] - 1 + 127, 0) - down, 1)
    scale = np.exp2(byte - 127.0)
    codes = (blocks / scale).astype(np.float32).astype(dtype).astype(np.float64)
    return np.moveaxis((codes * scale).reshape(v.shape), -1, axis)


WIDE = False


def mx_kscale(k):
    if not WIDE:
        return np.ones(k)
    levels = np.array([10, -10, 5, -5, 0])
    a = np.random.permutation(np.resize(levels, k // 512 * 4)).reshape(k // 512, 4)
    idx = np.arange(k)
    return np.exp2(a[idx // 512, idx % 128 // 32])


BF16 = ml_dtypes.bfloat16


def bf(x):
    return np.asarray(x, np.float32).astype(BF16)


def f64(x):
    return np.asarray(x).astype(np.float64)


N, D_FEAT, D_EMB, H = 16, 511, 512, 4
SEQ = D_FEAT + 1
EPS = 1e-5


def ln(x):
    m = x.mean(-1, keepdims=True)
    v = ((x - m) ** 2).mean(-1, keepdims=True)
    return (x - m) / np.sqrt(v + EPS)


def setup_inputs():
    s = mx_kscale(D_EMB)
    return {'Z': bf(0.5 + 1.5 * np.random.standard_normal((N, D_FEAT))),
            'feat_emb': bf(np.random.standard_normal((D_FEAT, D_EMB)) * 0.02 + 0.01),
            'label_token': bf(np.random.standard_normal((1, 1, D_EMB)) * 0.02 + 0.01),
            'g1': bf((1.0 + 0.1 * np.random.standard_normal(D_EMB)) * s),
            'be1': bf(0.1 * np.random.standard_normal(D_EMB) * s),
            'wk': bf(np.random.standard_normal((D_EMB, D_EMB)) / np.sqrt(D_EMB) / s[:, None]),
            'bk': bf(0.3 * np.random.standard_normal(D_EMB)),
            'wv': bf(np.random.standard_normal((D_EMB, D_EMB)) / np.sqrt(D_EMB) / s[:, None]),
            'bv': bf(0.3 * np.random.standard_normal(D_EMB))}


def reference(Z, feat_emb, label_token, g1, be1, wk, bk, wv, bv):
    n = Z.shape[0]
    zn = ln(f64(Z))
    x_feats = zn[..., None] * f64(feat_emb)[None]
    lab = np.broadcast_to(f64(label_token), (n, 1, D_EMB))
    x = np.concatenate([x_feats, lab], axis=1)
    xn = ln(x) * f64(g1) + f64(be1)
    xq = mxq(xn, 2, 'e4m3')
    k = (xq @ mxq(f64(wk), 0, 'e4m3')) + f64(bk)
    v = (xq @ mxq(f64(wv), 0, 'e4m3')) + f64(bv)
    return k, v

@@ -1,0 +1,230 @@
+from contextlib import ExitStack
+
+import concourse.mybir as mybir
+from concourse.masks import make_identity
+
+F32 = mybir.dt.float32
+BF16 = mybir.dt.bfloat16
+U32 = mybir.dt.uint32
+U8 = mybir.dt.uint8
+FP8X4 = mybir.dt.float8_e4m3fn_x4
+ALU = mybir.AluOpType
+ACT = mybir.ActivationFunctionType
+
+P = 128
+PACK = 4
+N_B = 16
+D_FEAT = 511
+SEQ = 512
+D_EMB = 512
+TILES = SEQ // P
+EPS = 1e-5
+
+FLOPS = 2 * N_B * SEQ * D_EMB * (2 * D_EMB)
+
+
+def tile_causalfeaturetransformer_pa_t_kernel(
+    tc, Z, feat_emb, label_token, g1, be1, wk, bk, wv, bv, out_0, out_1
+):
+    nc = tc.nc
+    weights = (wk, wv)
+    biases = (bk, bv)
+    out_views = tuple(o.rearrange("n (p j) e -> n p j e", j=TILES) for o in (out_0, out_1))
+
+    with ExitStack() as ctx:
+        keep = ctx.enter_context(tc.tile_pool(name="keep", bufs=1))
+        work = ctx.enter_context(tc.tile_pool(name="work", bufs=2))
+        results = ctx.enter_context(tc.tile_pool(name="results", bufs=3))
+        psum_t = ctx.enter_context(tc.psum_pool(name="psum_t", bufs=4))
+        psum_mx = ctx.enter_context(tc.psum_pool(name="psum_mx", bufs=4))
+
+        one_col = keep.tile([P, 1], F32)
+        nc.vector.memset(one_col[:], 1.0)
+        warm = keep.tile([P, 1], F32)
+        nc.scalar.activation(out=warm[:], in_=one_col[:], func=ACT.Sqrt)
+        ident_f32 = keep.tile([P, P], F32)
+        make_identity(nc, ident_f32[:])
+        ident_bf16 = keep.tile([P, P], BF16)
+        make_identity(nc, ident_bf16[:])
+
+        z_raw = keep.tile([N_B, SEQ], BF16)
+        nc.vector.memset(z_raw[:], 0.0)
+        nc.sync.dma_start(out=z_raw[:, 0:D_FEAT], in_=Z)
+
+        tokens = keep.tile([P, TILES, D_EMB], BF16)
+        nc.sync.dma_start(
+            out=tokens[0:112], in_=feat_emb[0:448].rearrange("(p j) d -> p j d", j=TILES)
+        )
+        nc.sync.dma_start(
+            out=tokens[112:127], in_=feat_emb[448:508].rearrange("(p j) d -> p j d", j=TILES)
+        )
+        nc.sync.dma_start(
+            out=tokens[127:128, 0:3, :], in_=feat_emb[508:511].rearrange("(p j) d -> p j d", p=1)
+        )
+        nc.sync.dma_start(out=tokens[127:128, 3:4, :], in_=label_token)
+
+        gain_rows = keep.tile([P, P], BF16)
+        nc.vector.memset(gain_rows[:], 0.0)
+        nc.scalar.dma_start(out=gain_rows[0:PACK, :], in_=g1.rearrange("(t q) -> t q", q=P))
+        nc.scalar.dma_start(out=gain_rows[PACK : 2 * PACK, :], in_=be1.rearrange("(t q) -> t q", q=P))
+
+        w_raw = []
+        for o in range(2):
+            raw = keep.tile([P, PACK, D_EMB], BF16, name="w_raw%d" % o)
+            nc.sync.dma_start(out=raw[:], in_=weights[o].rearrange("(t q) e -> q t e", q=P))
+            w_raw.append(raw)
+
+        bias_all = keep.tile([P, 2, D_EMB], BF16)
+        for o in range(2):
+            nc.scalar.dma_start(out=bias_all[:, o, :], in_=biases[o].partition_broadcast(P))
+
+        z_stats = keep.tile([N_B, 6], F32)
+        nc.vector.bn_stats(out=z_stats[:], in_=z_raw[:, 0:D_FEAT])
+        z_mv = keep.tile([N_B, 2], F32)
+        nc.vector.bn_aggr(out=z_mv[:], in_=z_stats[:])
+        z_var_eps = keep.tile([N_B, 1], F32)
+        nc.vector.tensor_scalar(
+            out=z_var_eps[:], in0=z_mv[:, 1:2], scalar1=EPS, scalar2=None, op0=ALU.add
+        )
+        z_sd = keep.tile([N_B, 1], F32)
+        nc.scalar.activation(out=z_sd[:], in_=z_var_eps[:], func=ACT.Sqrt)
+        z_rstd = keep.tile([N_B, 1], F32)
+        nc.vector.reciprocal(out=z_rstd[:], in_=z_sd[:])
+        zn_rows = keep.tile([P, SEQ], F32)
+        nc.vector.memset(zn_rows[:], 0.0)
+        nc.vector.tensor_scalar(
+            out=zn_rows[0:N_B, :].rearrange("n (j p) -> n j p", j=TILES),
+            in0=z_raw[:].rearrange("n (p j) -> n j p", j=TILES),
+            scalar1=z_mv[:, 0:1],
+            scalar2=z_rstd[:],
+            op0=ALU.subtract,
+            op1=ALU.mult,
+        )
+        nc.vector.memset(zn_rows[0:N_B, SEQ - 1 : SEQ], 1.0)
+        zn_psum = psum_t.tile([P, TILES, P], F32, tag="t")
+        for j in range(TILES):
+            nc.tensor.transpose(zn_psum[:, j, :], zn_rows[:, j * P : (j + 1) * P], ident_f32[:])
+        zn_cols = keep.tile([P, TILES, N_B], F32)
+        nc.vector.tensor_copy(out=zn_cols[:], in_=zn_psum[:, :, 0:N_B])
+
+        tok_stats = keep.tile([P, TILES, 6], F32)
+        tok_mv = keep.tile([P, TILES, 2], F32)
+        for j in range(TILES):
+            nc.vector.bn_stats(out=tok_stats[:, j, :], in_=tokens[:, j, :])
+            nc.vector.bn_aggr(out=tok_mv[:, j, :], in_=tok_stats[:, j, :])
+        neg_mean = keep.tile([P, TILES, 1], F32)
+        nc.vector.tensor_scalar(
+            out=neg_mean[:], in0=tok_mv[:, :, 0:1], scalar1=-1.0, scalar2=None, op0=ALU.mult
+        )
+
+        shape_c = [P, TILES, N_B]
+        zn_sq = keep.tile(shape_c, F32)
+        nc.vector.tensor_tensor(out=zn_sq[:], in0=zn_cols[:], in1=zn_cols[:], op=ALU.mult)
+        x_var = keep.tile(shape_c, F32)
+        nc.vector.tensor_tensor(
+            out=x_var[:], in0=zn_sq[:], in1=tok_mv[:, :, 1:2].to_broadcast(shape_c), op=ALU.mult
+        )
+        x_var_eps = keep.tile(shape_c, F32)
+        nc.vector.tensor_scalar(
+            out=x_var_eps[:], in0=x_var[:], scalar1=EPS, scalar2=None, op0=ALU.add
+        )
+        x_sd = keep.tile(shape_c, F32)
+        nc.scalar.activation(out=x_sd[:], in_=x_var_eps[:], func=ACT.Sqrt)
+        x_rstd = keep.tile(shape_c, F32)
+        nc.vector.reciprocal(out=x_rstd[:], in_=x_sd[:])
+        c_scale = keep.tile(shape_c, F32)
+        nc.vector.tensor_tensor(out=c_scale[:], in0=zn_cols[:], in1=x_rstd[:], op=ALU.mult)
+        c_shift = keep.tile(shape_c, F32)
+        nc.vector.tensor_tensor(
+            out=c_shift[:], in0=c_scale[:], in1=neg_mean[:].to_broadcast(shape_c), op=ALU.mult
+        )
+
+        gain_psum = psum_t.tile([P, P], BF16, tag="t")
+        nc.tensor.transpose(gain_psum[:], gain_rows[:], ident_bf16[:])
+        gain_cols = keep.tile([P, 2 * PACK], F32)
+        nc.vector.tensor_copy(out=gain_cols[:], in_=gain_psum[:, 0 : 2 * PACK])
+
+        w_codes = []
+        w_scales = []
+        for o in range(2):
+            grouped_w = keep.tile([P, D_EMB, PACK], BF16, name="w_grouped%d" % o, align_bytes=64)
+            nc.gpsimd.tensor_scalar(
+                out=grouped_w[:],
+                in0=w_raw[o][:].rearrange("q t e -> q e t"),
+                scalar1=1.0,
+                scalar2=0.0,
+                op0=ALU.mult,
+                op1=ALU.add,
+            )
+            codes_w = keep.tile([P, D_EMB], U32, name="w_codes%d" % o, align_bytes=64)
+            scales_w = keep.tile([P, D_EMB], U8, name="w_scales%d" % o, align_bytes=64)
+            nc.vector.quantize_mx(
+                out=codes_w[:].bitcast(FP8X4),
+                scales=scales_w[:],
+                in_=grouped_w[:].rearrange("q e t -> q (e t)"),
+            )
+            w_codes.append(codes_w)
+            w_scales.append(scales_w)
+
+        for n in range(N_B):
+            z = work.tile([P, TILES, D_EMB], F32)
+            for j in range(TILES):
+                nc.scalar.activation(
+                    out=z[:, j, :],
+                    in_=tokens[:, j, :],
+                    func=ACT.Identity,
+                    scale=c_scale[:, j, n : n + 1],
+                    bias=c_shift[:, j, n : n + 1],
+                )
+            planes = work.tile([P, PACK, SEQ], BF16)
+            for t in range(PACK):
+                z_t = psum_t.tile([P, SEQ], F32, tag="t")
+                for j in range(TILES):
+                    nc.tensor.transpose(
+                        z_t[:, j * P : (j + 1) * P], z[:, j, t * P : (t + 1) * P], ident_f32[:]
+                    )
+                nc.scalar.activation(
+                    out=planes[:, t, :],
+                    in_=z_t[:],
+                    func=ACT.Identity,
+                    scale=gain_cols[:, t : t + 1],
+                    bias=gain_cols[:, PACK + t : PACK + t + 1],
+                )
+            grouped = work.tile([P, SEQ, PACK], BF16, align_bytes=64)
+            nc.gpsimd.tensor_scalar(
+                out=grouped[:],
+                in0=planes[:].rearrange("q t w -> q w t"),
+                scalar1=1.0,
+                scalar2=0.0,
+                op0=ALU.mult,
+                op1=ALU.add,
+            )
+            codes = work.tile([P, SEQ], U32, align_bytes=64)
+            scales = work.tile([P, SEQ], U8, align_bytes=64)
+            nc.vector.quantize_mx(
+                out=codes[:].bitcast(FP8X4),
+                scales=scales[:],
+                in_=grouped[:].rearrange("q w t -> q (w t)"),
+            )
+            res = [results.tile([P, TILES, D_EMB], F32, name="res%d" % o) for o in range(2)]
+            for j in range(TILES):
+                cols = slice(j * P, (j + 1) * P)
+                for o in range(2):
+                    acc = psum_mx.tile([P, D_EMB], F32)
+                    nc.tensor.matmul_mx(
+                        out=acc[:],
+                        lhsT=codes[:, cols].bitcast(FP8X4),
+                        lhsT_scale=scales[:, cols],
+                        rhs=w_codes[o][:].bitcast(FP8X4),
+                        rhs_scale=w_scales[o][:],
+                        start=True,
+                        stop=True,
+                    )
+                    nc.vector.tensor_tensor(
+                        out=res[o][:, j, :], in0=acc[:], in1=bias_all[:, o, :], op=ALU.add
+                    )
+                if j % 2 == 1:
+                    for o in range(2):
+                        nc.sync.dma_start(
+                            out=out_views[o][n][:, j - 1 : j + 1, :], in_=res[o][:, j - 1 : j + 1, :]
+                        )

@@ -19,6 +19,7 @@ SEQ = 512
 D_EMB = 512
 TILES = SEQ // P
 EPS = 1e-5
+QUANT_AFTER = 6
 
 FLOPS = 2 * N_B * SEQ * D_EMB * (2 * D_EMB)
 
@@ -32,6 +33,7 @@ def tile_causalfeaturetransformer_pa_t_kernel(
     out_views = tuple(o.rearrange("n (p j) e -> n p j e", j=TILES) for o in (out_0, out_1))
 
     with ExitStack() as ctx:
+        ctx.enter_context(tc.manual_schedule())
         keep = ctx.enter_context(tc.tile_pool(name="keep", bufs=1))
         work = ctx.enter_context(tc.tile_pool(name="work", bufs=2))
         results = ctx.enter_context(tc.tile_pool(name="results", bufs=3))
@@ -78,6 +80,12 @@ def tile_causalfeaturetransformer_pa_t_kernel(
         for o in range(2):
             nc.scalar.dma_start(out=bias_all[:, o, :], in_=biases[o].partition_broadcast(P))
 
+        zn_rows = keep.tile([P, SEQ], F32)
+        nc.vector.memset(zn_rows[:], 0.0)
+
+        gain_psum = psum_t.tile([P, P], BF16, tag="t")
+        nc.tensor.transpose(gain_psum[:], gain_rows[:], ident_bf16[:])
+
         z_stats = keep.tile([N_B, 6], F32)
         nc.vector.bn_stats(out=z_stats[:], in_=z_raw[:, 0:D_FEAT])
         z_mv = keep.tile([N_B, 2], F32)
@@ -90,8 +98,6 @@ def tile_causalfeaturetransformer_pa_t_kernel(
         nc.scalar.activation(out=z_sd[:], in_=z_var_eps[:], func=ACT.Sqrt)
         z_rstd = keep.tile([N_B, 1], F32)
         nc.vector.reciprocal(out=z_rstd[:], in_=z_sd[:])
-        zn_rows = keep.tile([P, SEQ], F32)
-        nc.vector.memset(zn_rows[:], 0.0)
         nc.vector.tensor_scalar(
             out=zn_rows[0:N_B, :].rearrange("n (j p) -> n j p", j=TILES),
             in0=z_raw[:].rearrange("n (p j) -> n j p", j=TILES),
@@ -104,8 +110,6 @@ def tile_causalfeaturetransformer_pa_t_kernel(
         zn_psum = psum_t.tile([P, TILES, P], F32, tag="t")
         for j in range(TILES):
             nc.tensor.transpose(zn_psum[:, j, :], zn_rows[:, j * P : (j + 1) * P], ident_f32[:])
-        zn_cols = keep.tile([P, TILES, N_B], F32)
-        nc.vector.tensor_copy(out=zn_cols[:], in_=zn_psum[:, :, 0:N_B])
 
         tok_stats = keep.tile([P, TILES, 6], F32)
         tok_mv = keep.tile([P, TILES, 2], F32)
@@ -118,6 +122,8 @@ def tile_causalfeaturetransformer_pa_t_kernel(
         )
 
         shape_c = [P, TILES, N_B]
+        zn_cols = keep.tile(shape_c, F32)
+        nc.vector.tensor_copy(out=zn_cols[:], in_=zn_psum[:, :, 0:N_B])
         zn_sq = keep.tile(shape_c, F32)
         nc.vector.tensor_tensor(out=zn_sq[:], in0=zn_cols[:], in1=zn_cols[:], op=ALU.mult)
         x_var = keep.tile(shape_c, F32)
@@ -138,14 +144,10 @@ def tile_causalfeaturetransformer_pa_t_kernel(
         nc.vector.tensor_tensor(
             out=c_shift[:], in0=c_scale[:], in1=neg_mean[:].to_broadcast(shape_c), op=ALU.mult
         )
-
-        gain_psum = psum_t.tile([P, P], BF16, tag="t")
-        nc.tensor.transpose(gain_psum[:], gain_rows[:], ident_bf16[:])
         gain_cols = keep.tile([P, 2 * PACK], F32)
         nc.vector.tensor_copy(out=gain_cols[:], in_=gain_psum[:, 0 : 2 * PACK])
 
-        w_codes = []
-        w_scales = []
+        w_grouped = []
         for o in range(2):
             grouped_w = keep.tile([P, D_EMB, PACK], BF16, name="w_grouped%d" % o, align_bytes=64)
             nc.gpsimd.tensor_scalar(
@@ -156,27 +158,51 @@ def tile_causalfeaturetransformer_pa_t_kernel(
                 op0=ALU.mult,
                 op1=ALU.add,
             )
-            codes_w = keep.tile([P, D_EMB], U32, name="w_codes%d" % o, align_bytes=64)
-            scales_w = keep.tile([P, D_EMB], U8, name="w_scales%d" % o, align_bytes=64)
-            nc.vector.quantize_mx(
-                out=codes_w[:].bitcast(FP8X4),
-                scales=scales_w[:],
-                in_=grouped_w[:].rearrange("q e t -> q (e t)"),
-            )
-            w_codes.append(codes_w)
-            w_scales.append(scales_w)
+            w_grouped.append(grouped_w)
+        w_codes = []
+        w_scales = []
 
-        for n in range(N_B):
-            z = work.tile([P, TILES, D_EMB], F32)
-            for j in range(TILES):
-                nc.scalar.activation(
-                    out=z[:, j, :],
-                    in_=tokens[:, j, :],
-                    func=ACT.Identity,
-                    scale=c_scale[:, j, n : n + 1],
-                    bias=c_shift[:, j, n : n + 1],
+        def quantise_weights():
+            for o in range(2):
+                codes_w = keep.tile([P, D_EMB], U32, name="w_codes%d" % o, align_bytes=64)
+                scales_w = keep.tile([P, D_EMB], U8, name="w_scales%d" % o, align_bytes=64)
+                nc.vector.quantize_mx(
+                    out=codes_w[:].bitcast(FP8X4),
+                    scales=scales_w[:],
+                    in_=w_grouped[o][:].rearrange("q e t -> q (e t)"),
                 )
-            planes = work.tile([P, PACK, SEQ], BF16)
+                w_codes.append(codes_w)
+                w_scales.append(scales_w)
+
+        z_of = {}
+        grouped_of = {}
+        codes_of = {}
+
+        def scale_rows(n, on_vector=False):
+            z = work.tile([P, TILES, D_EMB], F32, name="z")
+            for j in range(TILES):
+                if on_vector:
+                    nc.vector.tensor_scalar(
+                        out=z[:, j, :],
+                        in0=tokens[:, j, :],
+                        scalar1=c_scale[:, j, n : n + 1],
+                        scalar2=c_shift[:, j, n : n + 1],
+                        op0=ALU.mult,
+                        op1=ALU.add,
+                    )
+                else:
+                    nc.scalar.activation(
+                        out=z[:, j, :],
+                        in_=tokens[:, j, :],
+                        func=ACT.Identity,
+                        scale=c_scale[:, j, n : n + 1],
+                        bias=c_shift[:, j, n : n + 1],
+                    )
+            z_of[n] = z
+
+        def normalise(n):
+            z = z_of[n]
+            planes = work.tile([P, PACK, SEQ], BF16, name="planes")
             for t in range(PACK):
                 z_t = psum_t.tile([P, SEQ], F32, tag="t")
                 for j in range(TILES):
@@ -190,7 +216,7 @@ def tile_causalfeaturetransformer_pa_t_kernel(
                     scale=gain_cols[:, t : t + 1],
                     bias=gain_cols[:, PACK + t : PACK + t + 1],
                 )
-            grouped = work.tile([P, SEQ, PACK], BF16, align_bytes=64)
+            grouped = work.tile([P, SEQ, PACK], BF16, name="grouped", align_bytes=64)
             nc.gpsimd.tensor_scalar(
                 out=grouped[:],
                 in0=planes[:].rearrange("q t w -> q w t"),
@@ -199,18 +225,27 @@ def tile_causalfeaturetransformer_pa_t_kernel(
                 op0=ALU.mult,
                 op1=ALU.add,
             )
-            codes = work.tile([P, SEQ], U32, align_bytes=64)
-            scales = work.tile([P, SEQ], U8, align_bytes=64)
+            grouped_of[n] = grouped
+
+        def quantise(n):
+            codes = work.tile([P, SEQ], U32, name="codes", align_bytes=64)
+            scales = work.tile([P, SEQ], U8, name="scales", align_bytes=64)
             nc.vector.quantize_mx(
                 out=codes[:].bitcast(FP8X4),
                 scales=scales[:],
-                in_=grouped[:].rearrange("q w t -> q (w t)"),
+                in_=grouped_of[n][:].rearrange("q w t -> q (w t)"),
             )
+            codes_of[n] = (codes, scales)
+
+        def project(n):
+            codes, scales = codes_of[n]
             res = [results.tile([P, TILES, D_EMB], F32, name="res%d" % o) for o in range(2)]
             for j in range(TILES):
                 cols = slice(j * P, (j + 1) * P)
                 for o in range(2):
-                    acc = psum_mx.tile([P, D_EMB], F32)
+                    if 2 * j + o == QUANT_AFTER and n + 1 < N_B:
+                        quantise(n + 1)
+                    acc = psum_mx.tile([P, D_EMB], F32, name="acc")
                     nc.tensor.matmul_mx(
                         out=acc[:],
                         lhsT=codes[:, cols].bitcast(FP8X4),
@@ -228,3 +263,18 @@ def tile_causalfeaturetransformer_pa_t_kernel(
                         nc.sync.dma_start(
                             out=out_views[o][n][:, j - 1 : j + 1, :], in_=res[o][:, j - 1 : j + 1, :]
                         )
+
+        scale_rows(0)
+        scale_rows(1, on_vector=True)
+        quantise_weights()
+        normalise(0)
+        scale_rows(2)
+        normalise(1)
+        scale_rows(3)
+        quantise(0)
+        for n in range(N_B):
+            project(n)
+            if n + 2 < N_B:
+                normalise(n + 2)
+            if n + 4 < N_B:
+                scale_rows(n + 4)

@@ -19,7 +19,8 @@ SEQ = 512
 D_EMB = 512
 TILES = SEQ // P
 EPS = 1e-5
-QUANT_AFTER = 6
+BANKS = 2 * TILES
+QUANT_AFTER = 5
 
 FLOPS = 2 * N_B * SEQ * D_EMB * (2 * D_EMB)
 
@@ -243,7 +244,8 @@ def tile_causalfeaturetransformer_pa_t_kernel(
             for j in range(TILES):
                 cols = slice(j * P, (j + 1) * P)
                 for o in range(2):
-                    if 2 * j + o == QUANT_AFTER and n + 1 < N_B:
+                    bank = 2 * j + o
+                    if bank == QUANT_AFTER and n + 1 < N_B:
                         quantise(n + 1)
                     acc = psum_mx.tile([P, D_EMB], F32, name="acc")
                     nc.tensor.matmul_mx(
@@ -255,9 +257,16 @@ def tile_causalfeaturetransformer_pa_t_kernel(
                         start=True,
                         stop=True,
                     )
-                    nc.vector.tensor_tensor(
-                        out=res[o][:, j, :], in0=acc[:], in1=bias_all[:, o, :], op=ALU.add
-                    )
+                    if bank < BANKS - 1:
+                        nc.vector.tensor_tensor(
+                            out=res[o][:, j, :], in0=acc[:], in1=bias_all[:, o, :], op=ALU.add
+                        )
+                    else:
+                        bare = work.tile([P, D_EMB], F32, name="bare")
+                        nc.scalar.copy(out=bare[:], in_=acc[:])
+                        nc.gpsimd.tensor_tensor(
+                            out=res[o][:, j, :], in0=bare[:], in1=bias_all[:, o, :], op=ALU.add
+                        )
                 if j % 2 == 1:
                     for o in range(2):
                         nc.sync.dma_start(

@@ -19,8 +19,8 @@ SEQ = 512
 D_EMB = 512
 TILES = SEQ // P
 EPS = 1e-5
-BANKS = 2 * TILES
-QUANT_AFTER = 5
+QUANT_AFTER = 6
+AHEAD = 3
 
 FLOPS = 2 * N_B * SEQ * D_EMB * (2 * D_EMB)
 
@@ -180,7 +180,7 @@ def tile_causalfeaturetransformer_pa_t_kernel(
         codes_of = {}
 
         def scale_rows(n, on_vector=False):
-            z = work.tile([P, TILES, D_EMB], F32, name="z")
+            z = work.tile([P, TILES, D_EMB], F32, name="z", bufs=AHEAD + 1)
             for j in range(TILES):
                 if on_vector:
                     nc.vector.tensor_scalar(
@@ -217,7 +217,7 @@ def tile_causalfeaturetransformer_pa_t_kernel(
                     scale=gain_cols[:, t : t + 1],
                     bias=gain_cols[:, PACK + t : PACK + t + 1],
                 )
-            grouped = work.tile([P, SEQ, PACK], BF16, name="grouped", align_bytes=64)
+            grouped = work.tile([P, SEQ, PACK], BF16, name="grouped", bufs=AHEAD, align_bytes=64)
             nc.gpsimd.tensor_scalar(
                 out=grouped[:],
                 in0=planes[:].rearrange("q t w -> q w t"),
@@ -244,8 +244,7 @@ def tile_causalfeaturetransformer_pa_t_kernel(
             for j in range(TILES):
                 cols = slice(j * P, (j + 1) * P)
                 for o in range(2):
-                    bank = 2 * j + o
-                    if bank == QUANT_AFTER and n + 1 < N_B:
+                    if 2 * j + o == QUANT_AFTER and n + 1 < N_B:
                         quantise(n + 1)
                     acc = psum_mx.tile([P, D_EMB], F32, name="acc")
                     nc.tensor.matmul_mx(
@@ -257,16 +256,9 @@ def tile_causalfeaturetransformer_pa_t_kernel(
                         start=True,
                         stop=True,
                     )
-                    if bank < BANKS - 1:
-                        nc.vector.tensor_tensor(
-                            out=res[o][:, j, :], in0=acc[:], in1=bias_all[:, o, :], op=ALU.add
-                        )
-                    else:
-                        bare = work.tile([P, D_EMB], F32, name="bare")
-                        nc.scalar.copy(out=bare[:], in_=acc[:])
-                        nc.gpsimd.tensor_tensor(
-                            out=res[o][:, j, :], in0=bare[:], in1=bias_all[:, o, :], op=ALU.add
-                        )
+                    nc.vector.tensor_tensor(
+                        out=res[o][:, j, :], in0=acc[:], in1=bias_all[:, o, :], op=ALU.add
+                    )
                 if j % 2 == 1:
                     for o in range(2):
                         nc.sync.dma_start(
@@ -274,16 +266,16 @@ def tile_causalfeaturetransformer_pa_t_kernel(
                         )
 
         scale_rows(0)
-        scale_rows(1, on_vector=True)
+        for n in range(1, AHEAD + 1):
+            scale_rows(n, on_vector=True)
         quantise_weights()
-        normalise(0)
-        scale_rows(2)
-        normalise(1)
-        scale_rows(3)
+        for n in range(AHEAD):
+            normalise(n)
+        scale_rows(AHEAD + 1)
         quantise(0)
         for n in range(N_B):
             project(n)
-            if n + 2 < N_B:
-                normalise(n + 2)
-            if n + 4 < N_B:
-                scale_rows(n + 4)
+            if n + AHEAD < N_B:
+                normalise(n + AHEAD)
+            if n + AHEAD + 2 < N_B:
+                scale_rows(n + AHEAD + 2)

from contextlib import ExitStack

import concourse.mybir as mybir
from concourse.masks import make_identity

F32 = mybir.dt.float32
BF16 = mybir.dt.bfloat16
U32 = mybir.dt.uint32
U8 = mybir.dt.uint8
FP8X4 = mybir.dt.float8_e4m3fn_x4
ALU = mybir.AluOpType
ACT = mybir.ActivationFunctionType

P = 128
PACK = 4
N_B = 16
D_FEAT = 511
SEQ = 512
D_EMB = 512
TILES = SEQ // P
EPS = 1e-5
QUANT_AFTER = 6
AHEAD = 3

FLOPS = 2 * N_B * SEQ * D_EMB * (2 * D_EMB)


def tile_causalfeaturetransformer_pa_t_kernel(
    tc, Z, feat_emb, label_token, g1, be1, wk, bk, wv, bv, out_0, out_1
):
    nc = tc.nc
    weights = (wk, wv)
    biases = (bk, bv)
    out_views = tuple(o.rearrange("n (p j) e -> n p j e", j=TILES) for o in (out_0, out_1))

    with ExitStack() as ctx:
        ctx.enter_context(tc.manual_schedule())
        keep = ctx.enter_context(tc.tile_pool(name="keep", bufs=1))
        work = ctx.enter_context(tc.tile_pool(name="work", bufs=2))
        results = ctx.enter_context(tc.tile_pool(name="results", bufs=3))
        psum_t = ctx.enter_context(tc.psum_pool(name="psum_t", bufs=4))
        psum_mx = ctx.enter_context(tc.psum_pool(name="psum_mx", bufs=4))

        one_col = keep.tile([P, 1], F32)
        nc.vector.memset(one_col[:], 1.0)
        warm = keep.tile([P, 1], F32)
        nc.scalar.activation(out=warm[:], in_=one_col[:], func=ACT.Sqrt)
        ident_f32 = keep.tile([P, P], F32)
        make_identity(nc, ident_f32[:])
        ident_bf16 = keep.tile([P, P], BF16)
        make_identity(nc, ident_bf16[:])

        z_raw = keep.tile([N_B, SEQ], BF16)
        nc.vector.memset(z_raw[:], 0.0)
        nc.sync.dma_start(out=z_raw[:, 0:D_FEAT], in_=Z)

        tokens = keep.tile([P, TILES, D_EMB], BF16)
        nc.sync.dma_start(
            out=tokens[0:112], in_=feat_emb[0:448].rearrange("(p j) d -> p j d", j=TILES)
        )
        nc.sync.dma_start(
            out=tokens[112:127], in_=feat_emb[448:508].rearrange("(p j) d -> p j d", j=TILES)
        )
        nc.sync.dma_start(
            out=tokens[127:128, 0:3, :], in_=feat_emb[508:511].rearrange("(p j) d -> p j d", p=1)
        )
        nc.sync.dma_start(out=tokens[127:128, 3:4, :], in_=label_token)

        gain_rows = keep.tile([P, P], BF16)
        nc.vector.memset(gain_rows[:], 0.0)
        nc.scalar.dma_start(out=gain_rows[0:PACK, :], in_=g1.rearrange("(t q) -> t q", q=P))
        nc.scalar.dma_start(out=gain_rows[PACK : 2 * PACK, :], in_=be1.rearrange("(t q) -> t q", q=P))

        w_raw = []
        for o in range(2):
            raw = keep.tile([P, PACK, D_EMB], BF16, name="w_raw%d" % o)
            nc.sync.dma_start(out=raw[:], in_=weights[o].rearrange("(t q) e -> q t e", q=P))
            w_raw.append(raw)

        bias_all = keep.tile([P, 2, D_EMB], BF16)
        for o in range(2):
            nc.scalar.dma_start(out=bias_all[:, o, :], in_=biases[o].partition_broadcast(P))

        zn_rows = keep.tile([P, SEQ], F32)
        nc.vector.memset(zn_rows[:], 0.0)

        gain_psum = psum_t.tile([P, P], BF16, tag="t")
        nc.tensor.transpose(gain_psum[:], gain_rows[:], ident_bf16[:])

        z_stats = keep.tile([N_B, 6], F32)
        nc.vector.bn_stats(out=z_stats[:], in_=z_raw[:, 0:D_FEAT])
        z_mv = keep.tile([N_B, 2], F32)
        nc.vector.bn_aggr(out=z_mv[:], in_=z_stats[:])
        z_var_eps = keep.tile([N_B, 1], F32)
        nc.vector.tensor_scalar(
            out=z_var_eps[:], in0=z_mv[:, 1:2], scalar1=EPS, scalar2=None, op0=ALU.add
        )
        z_sd = keep.tile([N_B, 1], F32)
        nc.scalar.activation(out=z_sd[:], in_=z_var_eps[:], func=ACT.Sqrt)
        z_rstd = keep.tile([N_B, 1], F32)
        nc.vector.reciprocal(out=z_rstd[:], in_=z_sd[:])
        nc.vector.tensor_scalar(
            out=zn_rows[0:N_B, :].rearrange("n (j p) -> n j p", j=TILES),
            in0=z_raw[:].rearrange("n (p j) -> n j p", j=TILES),
            scalar1=z_mv[:, 0:1],
            scalar2=z_rstd[:],
            op0=ALU.subtract,
            op1=ALU.mult,
        )
        nc.vector.memset(zn_rows[0:N_B, SEQ - 1 : SEQ], 1.0)
        zn_psum = psum_t.tile([P, TILES, P], F32, tag="t")
        for j in range(TILES):
            nc.tensor.transpose(zn_psum[:, j, :], zn_rows[:, j * P : (j + 1) * P], ident_f32[:])

        tok_stats = keep.tile([P, TILES, 6], F32)
        tok_mv = keep.tile([P, TILES, 2], F32)
        for j in range(TILES):
            nc.vector.bn_stats(out=tok_stats[:, j, :], in_=tokens[:, j, :])
            nc.vector.bn_aggr(out=tok_mv[:, j, :], in_=tok_stats[:, j, :])
        neg_mean = keep.tile([P, TILES, 1], F32)
        nc.vector.tensor_scalar(
            out=neg_mean[:], in0=tok_mv[:, :, 0:1], scalar1=-1.0, scalar2=None, op0=ALU.mult
        )

        shape_c = [P, TILES, N_B]
        zn_cols = keep.tile(shape_c, F32)
        nc.vector.tensor_copy(out=zn_cols[:], in_=zn_psum[:, :, 0:N_B])
        zn_sq = keep.tile(shape_c, F32)
        nc.vector.tensor_tensor(out=zn_sq[:], in0=zn_cols[:], in1=zn_cols[:], op=ALU.mult)
        x_var = keep.tile(shape_c, F32)
        nc.vector.tensor_tensor(
            out=x_var[:], in0=zn_sq[:], in1=tok_mv[:, :, 1:2].to_broadcast(shape_c), op=ALU.mult
        )
        x_var_eps = keep.tile(shape_c, F32)
        nc.vector.tensor_scalar(
            out=x_var_eps[:], in0=x_var[:], scalar1=EPS, scalar2=None, op0=ALU.add
        )
        x_sd = keep.tile(shape_c, F32)
        nc.scalar.activation(out=x_sd[:], in_=x_var_eps[:], func=ACT.Sqrt)
        x_rstd = keep.tile(shape_c, F32)
        nc.vector.reciprocal(out=x_rstd[:], in_=x_sd[:])
        c_scale = keep.tile(shape_c, F32)
        nc.vector.tensor_tensor(out=c_scale[:], in0=zn_cols[:], in1=x_rstd[:], op=ALU.mult)
        c_shift = keep.tile(shape_c, F32)
        nc.vector.tensor_tensor(
            out=c_shift[:], in0=c_scale[:], in1=neg_mean[:].to_broadcast(shape_c), op=ALU.mult
        )
        gain_cols = keep.tile([P, 2 * PACK], F32)
        nc.vector.tensor_copy(out=gain_cols[:], in_=gain_psum[:, 0 : 2 * PACK])

        w_grouped = []
        for o in range(2):
            grouped_w = keep.tile([P, D_EMB, PACK], BF16, name="w_grouped%d" % o, align_bytes=64)
            nc.gpsimd.tensor_scalar(
                out=grouped_w[:],
                in0=w_raw[o][:].rearrange("q t e -> q e t"),
                scalar1=1.0,
                scalar2=0.0,
                op0=ALU.mult,
                op1=ALU.add,
            )
            w_grouped.append(grouped_w)
        w_codes = []
        w_scales = []

        def quantise_weights():
            for o in range(2):
                codes_w = keep.tile([P, D_EMB], U32, name="w_codes%d" % o, align_bytes=64)
                scales_w = keep.tile([P, D_EMB], U8, name="w_scales%d" % o, align_bytes=64)
                nc.vector.quantize_mx(
                    out=codes_w[:].bitcast(FP8X4),
                    scales=scales_w[:],
                    in_=w_grouped[o][:].rearrange("q e t -> q (e t)"),
                )
                w_codes.append(codes_w)
                w_scales.append(scales_w)

        z_of = {}
        grouped_of = {}
        codes_of = {}

        def scale_rows(n, on_vector=False):
            z = work.tile([P, TILES, D_EMB], F32, name="z", bufs=AHEAD + 1)
            for j in range(TILES):
                if on_vector:
                    nc.vector.tensor_scalar(
                        out=z[:, j, :],
                        in0=tokens[:, j, :],
                        scalar1=c_scale[:, j, n : n + 1],
                        scalar2=c_shift[:, j, n : n + 1],
                        op0=ALU.mult,
                        op1=ALU.add,
                    )
                else:
                    nc.scalar.activation(
                        out=z[:, j, :],
                        in_=tokens[:, j, :],
                        func=ACT.Identity,
                        scale=c_scale[:, j, n : n + 1],
                        bias=c_shift[:, j, n : n + 1],
                    )
            z_of[n] = z

        def normalise(n):
            z = z_of[n]
            planes = work.tile([P, PACK, SEQ], BF16, name="planes")
            for t in range(PACK):
                z_t = psum_t.tile([P, SEQ], F32, tag="t")
                for j in range(TILES):
                    nc.tensor.transpose(
                        z_t[:, j * P : (j + 1) * P], z[:, j, t * P : (t + 1) * P], ident_f32[:]
                    )
                nc.scalar.activation(
                    out=planes[:, t, :],
                    in_=z_t[:],
                    func=ACT.Identity,
                    scale=gain_cols[:, t : t + 1],
                    bias=gain_cols[:, PACK + t : PACK + t + 1],
                )
            grouped = work.tile([P, SEQ, PACK], BF16, name="grouped", bufs=AHEAD, align_bytes=64)
            nc.gpsimd.tensor_scalar(
                out=grouped[:],
                in0=planes[:].rearrange("q t w -> q w t"),
                scalar1=1.0,
                scalar2=0.0,
                op0=ALU.mult,
                op1=ALU.add,
            )
            grouped_of[n] = grouped

        def quantise(n):
            codes = work.tile([P, SEQ], U32, name="codes", align_bytes=64)
            scales = work.tile([P, SEQ], U8, name="scales", align_bytes=64)
            nc.vector.quantize_mx(
                out=codes[:].bitcast(FP8X4),
                scales=scales[:],
                in_=grouped_of[n][:].rearrange("q w t -> q (w t)"),
            )
            codes_of[n] = (codes, scales)

        def project(n):
            codes, scales = codes_of[n]
            res = [results.tile([P, TILES, D_EMB], F32, name="res%d" % o) for o in range(2)]
            for j in range(TILES):
                cols = slice(j * P, (j + 1) * P)
                for o in range(2):
                    if 2 * j + o == QUANT_AFTER and n + 1 < N_B:
                        quantise(n + 1)
                    acc = psum_mx.tile([P, D_EMB], F32, name="acc")
                    nc.tensor.matmul_mx(
                        out=acc[:],
                        lhsT=codes[:, cols].bitcast(FP8X4),
                        lhsT_scale=scales[:, cols],
                        rhs=w_codes[o][:].bitcast(FP8X4),
                        rhs_scale=w_scales[o][:],
                        start=True,
                        stop=True,
                    )
                    nc.vector.tensor_tensor(
                        out=res[o][:, j, :], in0=acc[:], in1=bias_all[:, o, :], op=ALU.add
                    )
                if j % 2 == 1:
                    for o in range(2):
                        nc.sync.dma_start(
                            out=out_views[o][n][:, j - 1 : j + 1, :], in_=res[o][:, j - 1 : j + 1, :]
                        )

        scale_rows(0)
        for n in range(1, AHEAD + 1):
            scale_rows(n, on_vector=True)
        quantise_weights()
        for n in range(AHEAD):
            normalise(n)
        scale_rows(AHEAD + 1)
        quantise(0)
        for n in range(N_B):
            project(n)
            if n + AHEAD < N_B:
                normalise(n + AHEAD)
            if n + AHEAD + 2 < N_B:
                scale_rows(n + AHEAD + 2)
